import numpy as np
import ml_dtypes


def mxq(x, axis, fmt="e4m3"):
    dtype, down = {"e4m3": (ml_dtypes.float8_e4m3fn, 7), "e5m2": (ml_dtypes.float8_e5m2, 14)}[fmt]
    v = np.moveaxis(np.asarray(x, np.float32).astype(ml_dtypes.bfloat16).astype(np.float64), axis, -1)
    blocks = v.reshape(v.shape[:-1] + (-1, 32))
    amax = np.abs(blocks).max(-1, keepdims=True)
    byte = np.maximum(np.where(amax > 0, np.frexp(amax)[1] - 1 + 127, 0) - down, 1)
    scale = np.exp2(byte - 127.0)
    codes = (blocks / scale).astype(np.float32).astype(dtype).astype(np.float64)
    return np.moveaxis((codes * scale).reshape(v.shape), -1, axis)


WIDE = False


def mx_kscale(k):
    if not WIDE:
        return np.ones(k)
    levels = np.array([10, -10, 5, -5, 0])
    a = np.random.permutation(np.resize(levels, k // 512 * 4)).reshape(k // 512, 4)
    idx = np.arange(k)
    return np.exp2(a[idx // 512, idx % 128 // 32])


BF16 = ml_dtypes.bfloat16


def bf(x):
    return np.asarray(x, np.float32).astype(BF16)


def f64(x):
    return np.asarray(x).astype(np.float64)


B, N, D = 1, 2048, 512
P = 0.125
C = np.sqrt(4.0 / (3.0 * P * N))


def erf(v):
    u = np.clip(v, -6.0, 6.0)
    t = u.copy()
    acc = u.copy()
    for n in range(1, 121):
        t = t * (2.0 * u * u / (2.0 * n + 1.0))
        acc = acc + t
    return 2.0 / np.sqrt(np.pi) * np.exp(-u * u) * acc


def gelu(v):
    return 0.5 * v * (1.0 + erf(v / np.sqrt(2.0)))


def draw_adj():
    a = np.random.random((B, N, N)) * (np.random.random((B, N, N)) < P)
    return a * (np.random.random((B, N, 1)) > 0.05)


def setup_inputs():
    s = mx_kscale(D)
    return {"x": bf(np.random.standard_normal((B, N, D)) * s),
            "mask": bf(np.random.random((B, N)) > 0.2),
            "adj": bf(draw_adj()),
            "W0": bf(np.random.standard_normal((D, D)) * 0.7 / (C * np.sqrt(D)) / s),
            "b0": bf(np.random.standard_normal(D) * 0.3)}


def reference(x, mask, adj, W0, b0):
    a = f64(adj)
    deg = a.sum(-1)
    dinv = np.where(deg != 0, 1.0 / np.where(deg != 0, deg, 1.0), 0.0)
    adj_n = a * dinv[..., None]
    h = (mxq(f64(x), 2, "e4m3") @ mxq(f64(W0), 1, "e4m3").T) + f64(b0)
    z = mxq(adj_n, 2, "e4m3") @ mxq(h, 1, "e4m3")
    return gelu(z * f64(mask)[..., None])

@@ -1,0 +1,234 @@
+from contextlib import ExitStack
+
+import concourse.masks as masks
+import concourse.mybir as mybir
+
+F32 = mybir.dt.float32
+BF16 = mybir.dt.bfloat16
+U32 = mybir.dt.uint32
+U8 = mybir.dt.uint8
+FP8X4 = mybir.dt.float8_e4m3fn_x4
+ALU = mybir.AluOpType
+ACT = mybir.ActivationFunctionType
+
+P = 128
+PACK = 4
+K_PASS = P * PACK
+NODES = 2048
+FEAT = 512
+TILES = NODES // P
+PAIRS = TILES // 2
+PASSES = NODES // K_PASS
+SLAB = PACK * K_PASS
+
+SCALAR_PAIRS = 3
+AHEAD = 2
+
+FLOPS = 2 * NODES * FEAT * FEAT + 2 * NODES * NODES * FEAT
+
+
+def turn(nc, psum, stage, ident, slab):
+    words = slab.bitcast(F32)
+    grouped = stage.tile([P, PACK, P, PACK], BF16, tag="grouped", align_bytes=64)
+    for half in range(2):
+        bank = psum.tile([P, 4, P], F32, tag="turned")
+        for j in range(4):
+            first = (4 * half + j) * P
+            nc.tensor.transpose(bank[:, j, :], words[:, first : first + P], ident[:])
+        nc.scalar.copy(
+            out=grouped[:, 2 * half : 2 * half + 2].bitcast(F32),
+            in_=bank[:].rearrange("p (c u) r -> p c r u", u=2),
+        )
+    return grouped
+
+
+def quantise(nc, grouped, codes, scales):
+    nc.vector.quantize_mx(
+        out=codes.bitcast(FP8X4),
+        scales=scales,
+        in_=grouped[:].rearrange("p c r t -> p (c r t)"),
+    )
+
+
+def tile_graphconvlayer_pa_kernel(tc, x, mask, adj, W0, b0, out):
+    nc = tc.nc
+    adj_rows = adj[0].rearrange("(p i) m -> p i m", i=TILES)
+    out_rows = out[0].rearrange("(p i) o -> p i o", i=TILES)
+    mask_cols = mask[0].rearrange("(p i) -> p i", i=TILES)
+    x_rows = x[0].rearrange("(g q e) k -> q g (e k)", q=P, e=2)
+    w_rows = W0.rearrange("(a r) k -> r a k", r=P)
+
+    with ExitStack() as ctx:
+        const = ctx.enter_context(tc.tile_pool(name="const", bufs=1))
+        raw = ctx.enter_context(tc.tile_pool(name="raw", bufs=1))
+        stage = ctx.enter_context(tc.tile_pool(name="stage", bufs=4))
+        psum_turn = ctx.enter_context(tc.psum_pool(name="psum_turn", bufs=4))
+        psum_sum = ctx.enter_context(tc.psum_pool(name="psum_sum", bufs=4))
+        ctx.enter_context(tc.manual_schedule())
+
+        ident = const.tile([P, P], F32)
+        masks.make_identity(nc, ident[:])
+        ones = const.tile([P, P], BF16)
+        nc.vector.memset(ones[:], 1.0)
+        bias_row = const.tile([P, FEAT], BF16)
+        nc.vector.memset(bias_row[:], 0.0)
+        warm = const.tile([P, 1], F32)
+        nc.vector.memset(warm[:], 0.0)
+        nc.scalar.activation(out=warm[:], in_=warm[:], func=ACT.Gelu)
+
+        nc.sync.dma_start(out=bias_row[0:1, :], in_=b0.unsqueeze(0))
+        mask_bf = const.tile([P, TILES], BF16)
+        nc.sync.dma_start(out=mask_bf[:], in_=mask_cols)
+        w_raw = raw.tile([P, FEAT // P, FEAT], BF16)
+        nc.sync.dma_start(out=w_raw[:], in_=w_rows)
+        slabs = [w_raw[:].rearrange("p a k -> p (a k)")]
+        for c in range(PASSES):
+            x_piece = raw.tile([P, 2, 2 * FEAT], BF16, name="x_raw%d" % c)
+            nc.sync.dma_start(out=x_piece[:], in_=x_rows[:, 2 * c : 2 * c + 2, :])
+            slabs.append(x_piece[:].rearrange("p g k -> p (g k)"))
+        adj_raw = []
+        for r in range(PAIRS):
+            adj_pair = raw.tile([P, 2, NODES], BF16, name="adj_raw%d" % r)
+            nc.sync.dma_start(out=adj_pair[:], in_=adj_rows[:, 2 * r : 2 * r + 2, :])
+            adj_raw.append(adj_pair)
+
+        wx_codes = const.tile([P, 1 + PASSES, FEAT], U32, align_bytes=64)
+        wx_scales = const.tile([P, 1 + PASSES, FEAT], U8, align_bytes=64)
+        wx_grouped = []
+        for s in range(len(slabs) + 1):
+            if s < len(slabs):
+                wx_grouped.append(turn(nc, psum_turn, stage, ident, slabs[s]))
+            if s > 0:
+                quantise(nc, wx_grouped[s - 1], wx_codes[:, s - 1, :], wx_scales[:, s - 1, :])
+
+        bias_ps = psum_sum.tile([P, FEAT], F32, tag="sums")
+        nc.tensor.matmul(out=bias_ps[:], lhsT=ones[:], rhs=bias_row[:], start=True, stop=True)
+        bias_all = const.tile([P, FEAT], F32)
+        nc.scalar.copy(out=bias_all[:], in_=bias_ps[:])
+        mask_f = const.tile([P, TILES], F32)
+        nc.vector.tensor_copy(out=mask_f[:], in_=mask_bf[:])
+
+        deg = [const.tile([P, 2], F32, name="deg%d" % r) for r in range(PAIRS)]
+        for r in range(SCALAR_PAIRS):
+            for w in range(2):
+                unread_s = stage.tile([P, NODES], BF16, tag="unread_s", bufs=1)
+                nc.scalar.activation(
+                    out=unread_s[:],
+                    in_=adj_raw[r][:, w, :],
+                    func=ACT.Copy,
+                    accum_out=deg[r][:, w : w + 1],
+                )
+
+        h_codes = const.tile([P, PASSES, FEAT], U32, align_bytes=64)
+        h_scales = const.tile([P, PASSES, FEAT], U8, align_bytes=64)
+        for c in range(PASSES):
+            h_grouped = stage.tile([P, PACK, P, PACK], BF16, tag="grouped", align_bytes=64)
+            for f in range(FEAT // P):
+                cols = slice(f * P, (f + 1) * P)
+                h_ps = psum_sum.tile([P, PACK, P], F32, tag="sums")
+                for t in range(PACK):
+                    nodes = slice(t * P, (t + 1) * P)
+                    nc.tensor.matmul_mx(
+                        out=h_ps[:, t, :],
+                        lhsT=wx_codes[:, 1 + c, nodes].bitcast(FP8X4),
+                        lhsT_scale=wx_scales[:, 1 + c, nodes],
+                        rhs=wx_codes[:, 0, cols].bitcast(FP8X4),
+                        rhs_scale=wx_scales[:, 0, cols],
+                        start=True,
+                        stop=True,
+                    )
+                nc.vector.tensor_tensor(
+                    out=h_grouped[:, f],
+                    in0=h_ps[:].rearrange("p t o -> p o t"),
+                    in1=bias_all[:, cols].unsqueeze(2).to_broadcast([P, P, PACK]),
+                    op=ALU.add,
+                )
+            quantise(nc, h_grouped, h_codes[:, c, :], h_scales[:, c, :])
+
+        safe = const.tile([P, PAIRS, 2], F32)
+        rec = const.tile([P, PAIRS, 2], F32)
+        dinv = const.tile([P, PAIRS, 2], F32)
+        adj_n = {}
+        grouped = {}
+        codes = {}
+
+        def live(r):
+            return 0 <= r < PAIRS
+
+        def quantise_tile(r, w):
+            a_codes = stage.tile([P, PASSES, P], U32, tag="a_codes", align_bytes=64)
+            a_scales = stage.tile([P, PASSES, P], U8, tag="a_scales", align_bytes=64)
+            quantise(
+                nc,
+                grouped[r, w],
+                a_codes[:].rearrange("p c n -> p (c n)"),
+                a_scales[:].rearrange("p c n -> p (c n)"),
+            )
+            codes[r, w] = (a_codes, a_scales)
+
+        for i in range(-1, PAIRS + 1):
+            if live(i):
+                for w in range(2):
+                    grouped[i, w] = turn(nc, psum_turn, stage, ident, adj_n[i, w][:])
+            if live(i + 1):
+                nc.vector.scalar_tensor_tensor(
+                    out=safe[:, i + 1, :], in0=deg[i + 1][:], scalar=0.0, in1=deg[i + 1][:],
+                    op0=ALU.is_equal, op1=ALU.add,
+                )
+            if live(i - 1):
+                quantise_tile(i - 1, 0)
+            if live(i + 1):
+                nc.vector.reciprocal(out=rec[:, i + 1, :], in_=safe[:, i + 1, :])
+            if live(i - 1):
+                quantise_tile(i - 1, 1)
+            if live(i + 1):
+                nc.vector.scalar_tensor_tensor(
+                    out=dinv[:, i + 1, :], in0=deg[i + 1][:], scalar=0.0, in1=rec[:, i + 1, :],
+                    op0=ALU.not_equal, op1=ALU.mult,
+                )
+            if SCALAR_PAIRS <= i + AHEAD < PAIRS:
+                for w in range(2):
+                    unread_v = stage.tile([P, NODES], BF16, tag="unread_v", bufs=1)
+                    nc.vector.tensor_scalar(
+                        out=unread_v[:],
+                        in0=adj_raw[i + AHEAD][:, w, :],
+                        scalar1=1.0,
+                        scalar2=None,
+                        op0=ALU.mult,
+                        op1=ALU.add,
+                        accum_out=deg[i + AHEAD][:, w : w + 1],
+                    )
+            if live(i + 1):
+                for w in range(2):
+                    scaled = stage.tile([P, NODES], BF16, tag="adj_n")
+                    nc.vector.tensor_scalar(
+                        out=scaled[:],
+                        in0=adj_raw[i + 1][:, w, :],
+                        scalar1=dinv[:, i + 1, w : w + 1],
+                        scalar2=None,
+                        op0=ALU.mult,
+                    )
+                    adj_n[i + 1, w] = scaled
+            if live(i - 1):
+                for w in range(2):
+                    a_codes, a_scales = codes[i - 1, w]
+                    z_ps = psum_sum.tile([P, FEAT], F32, tag="sums")
+                    for c in range(PASSES):
+                        nc.tensor.matmul_mx(
+                            out=z_ps[:],
+                            lhsT=a_codes[:, c, :].bitcast(FP8X4),
+                            lhsT_scale=a_scales[:, c, :],
+                            rhs=h_codes[:, c, :].bitcast(FP8X4),
+                            rhs_scale=h_scales[:, c, :],
+                            start=(c == 0),
+                            stop=(c == PASSES - 1),
+                        )
+                    tile_index = 2 * (i - 1) + w
+                    result = stage.tile([P, FEAT], F32, tag="result")
+                    nc.scalar.activation(
+                        out=result[:],
+                        in_=z_ps[:],
+                        func=ACT.Gelu,
+                        scale=mask_f[:, tile_index : tile_index + 1],
+                    )
+                    nc.sync.dma_start(out=out_rows[:, tile_index, :], in_=result[:])

@@ -23,6 +23,8 @@ SLAB = PACK * K_PASS
 
 SCALAR_PAIRS = 3
 AHEAD = 2
+SCALAR_AHEAD = 3
+APART = 8
 
 FLOPS = 2 * NODES * FEAT * FEAT + 2 * NODES * NODES * FEAT
 
@@ -108,16 +110,38 @@ def tile_graphconvlayer_pa_kernel(tc, x, mask, adj, W0, b0, out):
         mask_f = const.tile([P, TILES], F32)
         nc.vector.tensor_copy(out=mask_f[:], in_=mask_bf[:])
 
-        deg = [const.tile([P, 2], F32, name="deg%d" % r) for r in range(PAIRS)]
-        for r in range(SCALAR_PAIRS):
+        deg = [const.tile([P, 2, APART], F32, name="deg%d" % r) for r in range(PAIRS)]
+
+        def on_scalar(r, w):
+            return r < SCALAR_PAIRS or (r % 2 == 1 and w == 1)
+
+        def sum_on_scalar(r):
             for w in range(2):
-                unread_s = stage.tile([P, NODES], BF16, tag="unread_s", bufs=1)
-                nc.scalar.activation(
-                    out=unread_s[:],
-                    in_=adj_raw[r][:, w, :],
-                    func=ACT.Copy,
-                    accum_out=deg[r][:, w : w + 1],
-                )
+                if on_scalar(r, w):
+                    unread_s = stage.tile([P, NODES], BF16, tag="unread_s", bufs=1)
+                    nc.scalar.activation(
+                        out=unread_s[:],
+                        in_=adj_raw[r][:, w, :],
+                        func=ACT.Copy,
+                        accum_out=deg[r][:, w, 0:1],
+                    )
+
+        def sum_on_vector(r):
+            for w in range(2):
+                if not on_scalar(r, w):
+                    unread_v = stage.tile([P, NODES], BF16, tag="unread_v", bufs=1)
+                    nc.vector.tensor_scalar(
+                        out=unread_v[:],
+                        in0=adj_raw[r][:, w, :],
+                        scalar1=1.0,
+                        scalar2=None,
+                        op0=ALU.mult,
+                        op1=ALU.add,
+                        accum_out=deg[r][:, w, 0:1],
+                    )
+
+        for r in range(SCALAR_PAIRS):
+            sum_on_scalar(r)
 
         h_codes = const.tile([P, PASSES, FEAT], U32, align_bytes=64)
         h_scales = const.tile([P, PASSES, FEAT], U8, align_bytes=64)
@@ -170,9 +194,11 @@ def tile_graphconvlayer_pa_kernel(tc, x, mask, adj, W0, b0, out):
             if live(i):
                 for w in range(2):
                     grouped[i, w] = turn(nc, psum_turn, stage, ident, adj_n[i, w][:])
+            if SCALAR_PAIRS <= i + SCALAR_AHEAD < PAIRS:
+                sum_on_scalar(i + SCALAR_AHEAD)
             if live(i + 1):
                 nc.vector.scalar_tensor_tensor(
-                    out=safe[:, i + 1, :], in0=deg[i + 1][:], scalar=0.0, in1=deg[i + 1][:],
+                    out=safe[:, i + 1, :], in0=deg[i + 1][:, :, 0], scalar=0.0, in1=deg[i + 1][:, :, 0],
                     op0=ALU.is_equal, op1=ALU.add,
                 )
             if live(i - 1):
@@ -183,21 +209,11 @@ def tile_graphconvlayer_pa_kernel(tc, x, mask, adj, W0, b0, out):
                 quantise_tile(i - 1, 1)
             if live(i + 1):
                 nc.vector.scalar_tensor_tensor(
-                    out=dinv[:, i + 1, :], in0=deg[i + 1][:], scalar=0.0, in1=rec[:, i + 1, :],
+                    out=dinv[:, i + 1, :], in0=deg[i + 1][:, :, 0], scalar=0.0, in1=rec[:, i + 1, :],
                     op0=ALU.not_equal, op1=ALU.mult,
                 )
             if SCALAR_PAIRS <= i + AHEAD < PAIRS:
-                for w in range(2):
-                    unread_v = stage.tile([P, NODES], BF16, tag="unread_v", bufs=1)
-                    nc.vector.tensor_scalar(
-                        out=unread_v[:],
-                        in0=adj_raw[i + AHEAD][:, w, :],
-                        scalar1=1.0,
-                        scalar2=None,
-                        op0=ALU.mult,
-                        op1=ALU.add,
-                        accum_out=deg[i + AHEAD][:, w : w + 1],
-                    )
+                sum_on_vector(i + AHEAD)
             if live(i + 1):
                 for w in range(2):
                     scaled = stage.tile([P, NODES], BF16, tag="adj_n")

@@ -23,7 +23,7 @@ SLAB = PACK * K_PASS
 
 SCALAR_PAIRS = 3
 AHEAD = 2
-SCALAR_AHEAD = 3
+SCALAR_AHEAD = 4
 APART = 8
 
 FLOPS = 2 * NODES * FEAT * FEAT + 2 * NODES * NODES * FEAT

@@ -21,9 +21,10 @@ PAIRS = TILES // 2
 PASSES = NODES // K_PASS
 SLAB = PACK * K_PASS
 
-SCALAR_PAIRS = 3
-AHEAD = 2
-SCALAR_AHEAD = 4
+SHARED_TILES = 10
+STAGE_BUFS = 6
+TURN_BANKS = 4
+SUM_BANKS = 4
 APART = 8
 
 FLOPS = 2 * NODES * FEAT * FEAT + 2 * NODES * NODES * FEAT
@@ -63,13 +64,15 @@ def tile_graphconvlayer_pa_kernel(tc, x, mask, adj, W0, b0, out):
     with ExitStack() as ctx:
         const = ctx.enter_context(tc.tile_pool(name="const", bufs=1))
         raw = ctx.enter_context(tc.tile_pool(name="raw", bufs=1))
-        stage = ctx.enter_context(tc.tile_pool(name="stage", bufs=4))
-        psum_turn = ctx.enter_context(tc.psum_pool(name="psum_turn", bufs=4))
-        psum_sum = ctx.enter_context(tc.psum_pool(name="psum_sum", bufs=4))
+        stage = ctx.enter_context(tc.tile_pool(name="stage", bufs=STAGE_BUFS))
+        psum_turn = ctx.enter_context(tc.psum_pool(name="psum_turn", bufs=TURN_BANKS))
+        psum_sum = ctx.enter_context(tc.psum_pool(name="psum_sum", bufs=SUM_BANKS))
         ctx.enter_context(tc.manual_schedule())
 
         ident = const.tile([P, P], F32)
         masks.make_identity(nc, ident[:])
+        ident_bf = const.tile([P, P], BF16)
+        masks.make_identity(nc, ident_bf[:])
         ones = const.tile([P, P], BF16)
         nc.vector.memset(ones[:], 1.0)
         bias_row = const.tile([P, FEAT], BF16)
@@ -94,157 +97,228 @@ def tile_graphconvlayer_pa_kernel(tc, x, mask, adj, W0, b0, out):
             nc.sync.dma_start(out=adj_pair[:], in_=adj_rows[:, 2 * r : 2 * r + 2, :])
             adj_raw.append(adj_pair)
 
+        def adj_tile(i):
+            return adj_raw[i // 2][:, i % 2, :]
+
         wx_codes = const.tile([P, 1 + PASSES, FEAT], U32, align_bytes=64)
         wx_scales = const.tile([P, 1 + PASSES, FEAT], U8, align_bytes=64)
-        wx_grouped = []
-        for s in range(len(slabs) + 1):
-            if s < len(slabs):
-                wx_grouped.append(turn(nc, psum_turn, stage, ident, slabs[s]))
-            if s > 0:
-                quantise(nc, wx_grouped[s - 1], wx_codes[:, s - 1, :], wx_scales[:, s - 1, :])
+        wx_grouped = {}
+
+        def turn_slab(s):
+            wx_grouped[s] = turn(nc, psum_turn, stage, ident, slabs[s])
+
+        def quantise_slab(s):
+            quantise(nc, wx_grouped[s], wx_codes[:, s, :], wx_scales[:, s, :])
+
+        deg = [const.tile([P, 2, APART], F32, name="deg%d" % r) for r in range(PAIRS)]
+        safe = const.tile([P, PAIRS, 2], F32)
+        rec = const.tile([P, PAIRS, 2], F32)
+        dinv = const.tile([P, PAIRS, 2], F32)
+
+        def deg_of(i):
+            return deg[i // 2][:, i % 2, 0:1]
+
+        def sum_on_tensor(i):
+            if i < SHARED_TILES and i % 2 == 1:
+                fold = psum_turn.tile([P, 4, P], F32, tag="turned", name="fold")
+                for j in range(NODES // P):
+                    nc.tensor.matmul(
+                        out=fold[:, 0, :],
+                        lhsT=ident_bf[:],
+                        rhs=adj_tile(i)[:, j * P : (j + 1) * P],
+                        start=(j == 0),
+                        stop=(j == NODES // P - 1),
+                    )
+                unread_f = stage.tile([P, P], F32, tag="unread_f", bufs=1)
+                nc.scalar.activation(out=unread_f[:], in_=fold[:, 0, :], func=ACT.Copy, accum_out=deg_of(i))
+
+        def sum_on_scalar(i):
+            if i < SHARED_TILES and i % 2 == 0:
+                unread_s = stage.tile([P, NODES], BF16, tag="unread_s", bufs=1)
+                nc.scalar.activation(out=unread_s[:], in_=adj_tile(i), func=ACT.Copy, accum_out=deg_of(i))
+
+        def sum_on_vector(i):
+            if SHARED_TILES <= i < TILES:
+                unread_v = stage.tile([P, NODES], BF16, tag="unread_v", bufs=1)
+                nc.vector.tensor_scalar(
+                    out=unread_v[:], in0=adj_tile(i), scalar1=1.0, scalar2=None,
+                    op0=ALU.mult, op1=ALU.add, accum_out=deg_of(i),
+                )
+
+        def dinv_step(r, step):
+            if not 0 <= r < PAIRS:
+                return
+            d = deg[r][:, :, 0]
+            if step == 0:
+                nc.vector.scalar_tensor_tensor(
+                    out=safe[:, r, :], in0=d, scalar=0.0, in1=d, op0=ALU.is_equal, op1=ALU.add
+                )
+            elif step == 1:
+                nc.vector.reciprocal(out=rec[:, r, :], in_=safe[:, r, :])
+            else:
+                nc.vector.scalar_tensor_tensor(
+                    out=dinv[:, r, :], in0=d, scalar=0.0, in1=rec[:, r, :], op0=ALU.not_equal, op1=ALU.mult
+                )
+
+        adj_n = {}
+        grouped = {}
+        codes = {}
+
+        def normalise(i):
+            if i < TILES:
+                scaled = stage.tile([P, NODES], BF16, tag="adj_n")
+                factor = dinv[:, i // 2, i % 2 : i % 2 + 1]
+                nc.vector.tensor_scalar(
+                    out=scaled[:], in0=adj_tile(i), scalar1=factor, scalar2=None, op0=ALU.mult
+                )
+                adj_n[i] = scaled
+
+        def turn_tile(i):
+            if i < TILES:
+                grouped[i] = turn(nc, psum_turn, stage, ident, adj_n[i][:])
+
+        def quantise_tile(i):
+            a_codes = stage.tile([P, PASSES, P], U32, tag="a_codes", align_bytes=64)
+            a_scales = stage.tile([P, PASSES, P], U8, tag="a_scales", align_bytes=64)
+            quantise(
+                nc,
+                grouped[i],
+                a_codes[:].rearrange("p c n -> p (c n)"),
+                a_scales[:].rearrange("p c n -> p (c n)"),
+            )
+            codes[i] = (a_codes, a_scales)
+
+        def multiply(i):
+            a_codes, a_scales = codes[i]
+            z_ps = psum_sum.tile([P, FEAT], F32, tag="sums")
+            for c in range(PASSES):
+                nc.tensor.matmul_mx(
+                    out=z_ps[:],
+                    lhsT=a_codes[:, c, :].bitcast(FP8X4),
+                    lhsT_scale=a_scales[:, c, :],
+                    rhs=h_codes[:, c, :].bitcast(FP8X4),
+                    rhs_scale=h_scales[:, c, :],
+                    start=(c == 0),
+                    stop=(c == PASSES - 1),
+                )
+            result = stage.tile([P, FEAT], F32, tag="result")
+            nc.scalar.activation(out=result[:], in_=z_ps[:], func=ACT.Gelu, scale=mask_f[:, i : i + 1])
+            nc.sync.dma_start(out=out_rows[:, i, :], in_=result[:])
+
+        h_codes = const.tile([P, PASSES, FEAT], U32, align_bytes=64)
+        h_scales = const.tile([P, PASSES, FEAT], U8, align_bytes=64)
+        h_grouped = {}
+
+        def h_block(c, f):
+            cols = slice(f * P, (f + 1) * P)
+            if f == 0:
+                h_grouped[c] = stage.tile([P, PACK, P, PACK], BF16, tag="grouped", name="h_grouped", align_bytes=64)
+            h_ps = psum_sum.tile([P, PACK, P], F32, tag="sums")
+            for t in range(PACK):
+                nodes = slice(t * P, (t + 1) * P)
+                nc.tensor.matmul_mx(
+                    out=h_ps[:, t, :],
+                    lhsT=wx_codes[:, 1 + c, nodes].bitcast(FP8X4),
+                    lhsT_scale=wx_scales[:, 1 + c, nodes],
+                    rhs=wx_codes[:, 0, cols].bitcast(FP8X4),
+                    rhs_scale=wx_scales[:, 0, cols],
+                    start=True,
+                    stop=True,
+                )
+            nc.vector.tensor_tensor(
+                out=h_grouped[c][:, f],
+                in0=h_ps[:].rearrange("p t o -> p o t"),
+                in1=bias_all[:, cols].unsqueeze(2).to_broadcast([P, P, PACK]),
+                op=ALU.add,
+            )
+
+        def quantise_h(c):
+            quantise(nc, h_grouped[c], h_codes[:, c, :], h_scales[:, c, :])
 
         bias_ps = psum_sum.tile([P, FEAT], F32, tag="sums")
         nc.tensor.matmul(out=bias_ps[:], lhsT=ones[:], rhs=bias_row[:], start=True, stop=True)
         bias_all = const.tile([P, FEAT], F32)
         nc.scalar.copy(out=bias_all[:], in_=bias_ps[:])
+        turn_slab(0)
+        turn_slab(1)
+        quantise_slab(0)
+        quantise_slab(1)
         mask_f = const.tile([P, TILES], F32)
+        turn_slab(2)
+        h_block(0, 0)
+        turn_slab(3)
+        quantise_slab(2)
+        h_block(0, 1)
+        turn_slab(4)
+        quantise_slab(3)
+        sum_on_scalar(0)
+        h_block(0, 2)
+        h_block(0, 3)
         nc.vector.tensor_copy(out=mask_f[:], in_=mask_bf[:])
-
-        deg = [const.tile([P, 2, APART], F32, name="deg%d" % r) for r in range(PAIRS)]
-
-        def on_scalar(r, w):
-            return r < SCALAR_PAIRS or (r % 2 == 1 and w == 1)
-
-        def sum_on_scalar(r):
-            for w in range(2):
-                if on_scalar(r, w):
-                    unread_s = stage.tile([P, NODES], BF16, tag="unread_s", bufs=1)
-                    nc.scalar.activation(
-                        out=unread_s[:],
-                        in_=adj_raw[r][:, w, :],
-                        func=ACT.Copy,
-                        accum_out=deg[r][:, w, 0:1],
-                    )
-
-        def sum_on_vector(r):
-            for w in range(2):
-                if not on_scalar(r, w):
-                    unread_v = stage.tile([P, NODES], BF16, tag="unread_v", bufs=1)
-                    nc.vector.tensor_scalar(
-                        out=unread_v[:],
-                        in0=adj_raw[r][:, w, :],
-                        scalar1=1.0,
-                        scalar2=None,
-                        op0=ALU.mult,
-                        op1=ALU.add,
-                        accum_out=deg[r][:, w, 0:1],
-                    )
-
-        for r in range(SCALAR_PAIRS):
-            sum_on_scalar(r)
-
-        h_codes = const.tile([P, PASSES, FEAT], U32, align_bytes=64)
-        h_scales = const.tile([P, PASSES, FEAT], U8, align_bytes=64)
-        for c in range(PASSES):
-            h_grouped = stage.tile([P, PACK, P, PACK], BF16, tag="grouped", align_bytes=64)
-            for f in range(FEAT // P):
-                cols = slice(f * P, (f + 1) * P)
-                h_ps = psum_sum.tile([P, PACK, P], F32, tag="sums")
-                for t in range(PACK):
-                    nodes = slice(t * P, (t + 1) * P)
-                    nc.tensor.matmul_mx(
-                        out=h_ps[:, t, :],
-                        lhsT=wx_codes[:, 1 + c, nodes].bitcast(FP8X4),
-                        lhsT_scale=wx_scales[:, 1 + c, nodes],
-                        rhs=wx_codes[:, 0, cols].bitcast(FP8X4),
-                        rhs_scale=wx_scales[:, 0, cols],
-                        start=True,
-                        stop=True,
-                    )
-                nc.vector.tensor_tensor(
-                    out=h_grouped[:, f],
-                    in0=h_ps[:].rearrange("p t o -> p o t"),
-                    in1=bias_all[:, cols].unsqueeze(2).to_broadcast([P, P, PACK]),
-                    op=ALU.add,
-                )
-            quantise(nc, h_grouped, h_codes[:, c, :], h_scales[:, c, :])
-
-        safe = const.tile([P, PAIRS, 2], F32)
-        rec = const.tile([P, PAIRS, 2], F32)
-        dinv = const.tile([P, PAIRS, 2], F32)
-        adj_n = {}
-        grouped = {}
-        codes = {}
-
-        def live(r):
-            return 0 <= r < PAIRS
-
-        def quantise_tile(r, w):
-            a_codes = stage.tile([P, PASSES, P], U32, tag="a_codes", align_bytes=64)
-            a_scales = stage.tile([P, PASSES, P], U8, tag="a_scales", align_bytes=64)
-            quantise(
-                nc,
-                grouped[r, w],
-                a_codes[:].rearrange("p c n -> p (c n)"),
-                a_scales[:].rearrange("p c n -> p (c n)"),
-            )
-            codes[r, w] = (a_codes, a_scales)
-
-        for i in range(-1, PAIRS + 1):
-            if live(i):
-                for w in range(2):
-                    grouped[i, w] = turn(nc, psum_turn, stage, ident, adj_n[i, w][:])
-            if SCALAR_PAIRS <= i + SCALAR_AHEAD < PAIRS:
-                sum_on_scalar(i + SCALAR_AHEAD)
-            if live(i + 1):
-                nc.vector.scalar_tensor_tensor(
-                    out=safe[:, i + 1, :], in0=deg[i + 1][:, :, 0], scalar=0.0, in1=deg[i + 1][:, :, 0],
-                    op0=ALU.is_equal, op1=ALU.add,
-                )
-            if live(i - 1):
-                quantise_tile(i - 1, 0)
-            if live(i + 1):
-                nc.vector.reciprocal(out=rec[:, i + 1, :], in_=safe[:, i + 1, :])
-            if live(i - 1):
-                quantise_tile(i - 1, 1)
-            if live(i + 1):
-                nc.vector.scalar_tensor_tensor(
-                    out=dinv[:, i + 1, :], in0=deg[i + 1][:, :, 0], scalar=0.0, in1=rec[:, i + 1, :],
-                    op0=ALU.not_equal, op1=ALU.mult,
-                )
-            if SCALAR_PAIRS <= i + AHEAD < PAIRS:
-                sum_on_vector(i + AHEAD)
-            if live(i + 1):
-                for w in range(2):
-                    scaled = stage.tile([P, NODES], BF16, tag="adj_n")
-                    nc.vector.tensor_scalar(
-                        out=scaled[:],
-                        in0=adj_raw[i + 1][:, w, :],
-                        scalar1=dinv[:, i + 1, w : w + 1],
-                        scalar2=None,
-                        op0=ALU.mult,
-                    )
-                    adj_n[i + 1, w] = scaled
-            if live(i - 1):
-                for w in range(2):
-                    a_codes, a_scales = codes[i - 1, w]
-                    z_ps = psum_sum.tile([P, FEAT], F32, tag="sums")
-                    for c in range(PASSES):
-                        nc.tensor.matmul_mx(
-                            out=z_ps[:],
-                            lhsT=a_codes[:, c, :].bitcast(FP8X4),
-                            lhsT_scale=a_scales[:, c, :],
-                            rhs=h_codes[:, c, :].bitcast(FP8X4),
-                            rhs_scale=h_scales[:, c, :],
-                            start=(c == 0),
-                            stop=(c == PASSES - 1),
-                        )
-                    tile_index = 2 * (i - 1) + w
-                    result = stage.tile([P, FEAT], F32, tag="result")
-                    nc.scalar.activation(
-                        out=result[:],
-                        in_=z_ps[:],
-                        func=ACT.Gelu,
-                        scale=mask_f[:, tile_index : tile_index + 1],
-                    )
-                    nc.sync.dma_start(out=out_rows[:, tile_index, :], in_=result[:])
+        h_block(1, 0)
+        quantise_h(0)
+        sum_on_tensor(1)
+        sum_on_scalar(2)
+        h_block(1, 1)
+        quantise_slab(4)
+        h_block(1, 2)
+        h_block(1, 3)
+        h_block(2, 0)
+        quantise_h(1)
+        sum_on_tensor(3)
+        sum_on_scalar(4)
+        dinv_step(0, 0)
+        h_block(2, 1)
+        dinv_step(0, 1)
+        h_block(2, 2)
+        dinv_step(0, 2)
+        h_block(2, 3)
+        normalise(0)
+        h_block(3, 0)
+        normalise(1)
+        quantise_h(2)
+        sum_on_tensor(5)
+        h_block(3, 1)
+        dinv_step(1, 0)
+        sum_on_scalar(6)
+        turn_tile(0)
+        h_block(3, 2)
+        dinv_step(1, 1)
+        h_block(3, 3)
+        sum_on_tensor(7)
+        turn_tile(1)
+        sum_on_scalar(8)
+        dinv_step(1, 2)
+        quantise_h(3)
+        dinv_step(2, 0)
+        sum_on_tensor(9)
+        quantise_tile(0)
+        dinv_step(2, 1)
+        normalise(2)
+        dinv_step(2, 2)
+        normalise(3)
+        multiply(0)
+        quantise_tile(1)
+        dinv_step(3, 0)
+        normalise(4)
+        dinv_step(3, 1)
+        normalise(5)
+        turn_tile(2)
+        turn_tile(3)
+        multiply(1)
+        turn_tile(4)
+        turn_tile(5)
+        for i in range(2, TILES, 2):
+            quantise_tile(i)
+            dinv_step(i // 2 + 2, 2)
+            sum_on_vector(i + 7)
+            normalise(i + 4)
+            dinv_step(i // 2 + 3, 0)
+            quantise_tile(i + 1)
+            sum_on_vector(i + 8)
+            dinv_step(i // 2 + 3, 1)
+            normalise(i + 5)
+            multiply(i)
+            multiply(i + 1)
+            turn_tile(i + 4)
+            turn_tile(i + 5)

@@ -22,6 +22,9 @@ PASSES = NODES // K_PASS
 SLAB = PACK * K_PASS
 
 SHARED_TILES = 10
+ON_SCALAR = (0, 2, 4, 6, 13)
+ON_TENSOR = (1, 3, 5, 7, 9)
+FIRST = 0
 STAGE_BUFS = 6
 TURN_BANKS = 4
 SUM_BANKS = 4
@@ -82,20 +85,32 @@ def tile_graphconvlayer_pa_kernel(tc, x, mask, adj, W0, b0, out):
         nc.scalar.activation(out=warm[:], in_=warm[:], func=ACT.Gelu)
 
         nc.sync.dma_start(out=bias_row[0:1, :], in_=b0.unsqueeze(0))
-        mask_bf = const.tile([P, TILES], BF16)
-        nc.sync.dma_start(out=mask_bf[:], in_=mask_cols)
+        adj_raw = []
+
+        def load_pair(r, pieces=1):
+            adj_pair = raw.tile([P, 2, NODES], BF16, name="adj_raw%d" % r)
+            for w in range(pieces):
+                part = slice(2 * w // pieces, 2 * (w + 1) // pieces)
+                nc.sync.dma_start(
+                    out=adj_pair[:, part], in_=adj_rows[:, 2 * r + part.start : 2 * r + part.stop, :]
+                )
+            adj_raw.append(adj_pair)
+
+        for r in range(FIRST):
+            load_pair(r, 2)
         w_raw = raw.tile([P, FEAT // P, FEAT], BF16)
-        nc.sync.dma_start(out=w_raw[:], in_=w_rows)
+        for half in range(2):
+            nc.sync.dma_start(out=w_raw[:, 2 * half : 2 * half + 2], in_=w_rows[:, 2 * half : 2 * half + 2, :])
         slabs = [w_raw[:].rearrange("p a k -> p (a k)")]
         for c in range(PASSES):
             x_piece = raw.tile([P, 2, 2 * FEAT], BF16, name="x_raw%d" % c)
-            nc.sync.dma_start(out=x_piece[:], in_=x_rows[:, 2 * c : 2 * c + 2, :])
+            for u in range(2):
+                nc.sync.dma_start(out=x_piece[:, u], in_=x_rows[:, 2 * c + u, :])
             slabs.append(x_piece[:].rearrange("p g k -> p (g k)"))
-        adj_raw = []
-        for r in range(PAIRS):
-            adj_pair = raw.tile([P, 2, NODES], BF16, name="adj_raw%d" % r)
-            nc.sync.dma_start(out=adj_pair[:], in_=adj_rows[:, 2 * r : 2 * r + 2, :])
-            adj_raw.append(adj_pair)
+        mask_bf = const.tile([P, TILES], BF16)
+        nc.sync.dma_start(out=mask_bf[:], in_=mask_cols)
+        for r in range(FIRST, PAIRS):
+            load_pair(r)
 
         def adj_tile(i):
             return adj_raw[i // 2][:, i % 2, :]
@@ -112,14 +127,13 @@ def tile_graphconvlayer_pa_kernel(tc, x, mask, adj, W0, b0, out):
 
         deg = [const.tile([P, 2, APART], F32, name="deg%d" % r) for r in range(PAIRS)]
         safe = const.tile([P, PAIRS, 2], F32)
-        rec = const.tile([P, PAIRS, 2], F32)
         dinv = const.tile([P, PAIRS, 2], F32)
 
         def deg_of(i):
             return deg[i // 2][:, i % 2, 0:1]
 
         def sum_on_tensor(i):
-            if i < SHARED_TILES and i % 2 == 1:
+            if i in ON_TENSOR:
                 fold = psum_turn.tile([P, 4, P], F32, tag="turned", name="fold")
                 for j in range(NODES // P):
                     nc.tensor.matmul(
@@ -133,12 +147,12 @@ def tile_graphconvlayer_pa_kernel(tc, x, mask, adj, W0, b0, out):
                 nc.scalar.activation(out=unread_f[:], in_=fold[:, 0, :], func=ACT.Copy, accum_out=deg_of(i))
 
         def sum_on_scalar(i):
-            if i < SHARED_TILES and i % 2 == 0:
+            if i in ON_SCALAR:
                 unread_s = stage.tile([P, NODES], BF16, tag="unread_s", bufs=1)
                 nc.scalar.activation(out=unread_s[:], in_=adj_tile(i), func=ACT.Copy, accum_out=deg_of(i))
 
         def sum_on_vector(i):
-            if SHARED_TILES <= i < TILES:
+            if i < TILES and i not in ON_SCALAR and i not in ON_TENSOR:
                 unread_v = stage.tile([P, NODES], BF16, tag="unread_v", bufs=1)
                 nc.vector.tensor_scalar(
                     out=unread_v[:], in0=adj_tile(i), scalar1=1.0, scalar2=None,
@@ -154,11 +168,7 @@ def tile_graphconvlayer_pa_kernel(tc, x, mask, adj, W0, b0, out):
                     out=safe[:, r, :], in0=d, scalar=0.0, in1=d, op0=ALU.is_equal, op1=ALU.add
                 )
             elif step == 1:
-                nc.vector.reciprocal(out=rec[:, r, :], in_=safe[:, r, :])
-            else:
-                nc.vector.scalar_tensor_tensor(
-                    out=dinv[:, r, :], in0=d, scalar=0.0, in1=rec[:, r, :], op0=ALU.not_equal, op1=ALU.mult
-                )
+                nc.vector.reciprocal(out=dinv[:, r, :], in_=safe[:, r, :])
 
         adj_n = {}
         grouped = {}
@@ -190,20 +200,23 @@ def tile_graphconvlayer_pa_kernel(tc, x, mask, adj, W0, b0, out):
 
         def multiply(i):
             a_codes, a_scales = codes[i]
-            z_ps = psum_sum.tile([P, FEAT], F32, tag="sums")
-            for c in range(PASSES):
-                nc.tensor.matmul_mx(
-                    out=z_ps[:],
-                    lhsT=a_codes[:, c, :].bitcast(FP8X4),
-                    lhsT_scale=a_scales[:, c, :],
-                    rhs=h_codes[:, c, :].bitcast(FP8X4),
-                    rhs_scale=h_scales[:, c, :],
-                    start=(c == 0),
-                    stop=(c == PASSES - 1),
-                )
-            result = stage.tile([P, FEAT], F32, tag="result")
-            nc.scalar.activation(out=result[:], in_=z_ps[:], func=ACT.Gelu, scale=mask_f[:, i : i + 1])
-            nc.sync.dma_start(out=out_rows[:, i, :], in_=result[:])
+            pieces = 2 if i == TILES - 1 else 1
+            for piece in range(pieces):
+                cols = slice(piece * FEAT // pieces, (piece + 1) * FEAT // pieces)
+                z_ps = psum_sum.tile([P, FEAT // pieces], F32, tag="sums")
+                for c in range(PASSES):
+                    nc.tensor.matmul_mx(
+                        out=z_ps[:],
+                        lhsT=a_codes[:, c, :].bitcast(FP8X4),
+                        lhsT_scale=a_scales[:, c, :],
+                        rhs=h_codes[:, c, cols].bitcast(FP8X4),
+                        rhs_scale=h_scales[:, c, cols],
+                        start=(c == 0),
+                        stop=(c == PASSES - 1),
+                    )
+                result = stage.tile([P, FEAT // pieces], F32, tag="result")
+                nc.scalar.activation(out=result[:], in_=z_ps[:], func=ACT.Gelu, scale=mask_f[:, i : i + 1])
+                nc.sync.dma_start(out=out_rows[:, i, cols], in_=result[:])
 
         h_codes = const.tile([P, PASSES, FEAT], U32, align_bytes=64)
         h_scales = const.tile([P, PASSES, FEAT], U8, align_bytes=64)
@@ -240,15 +253,15 @@ def tile_graphconvlayer_pa_kernel(tc, x, mask, adj, W0, b0, out):
         bias_all = const.tile([P, FEAT], F32)
         nc.scalar.copy(out=bias_all[:], in_=bias_ps[:])
         turn_slab(0)
-        turn_slab(1)
         quantise_slab(0)
+        turn_slab(1)
         quantise_slab(1)
         mask_f = const.tile([P, TILES], F32)
         turn_slab(2)
         h_block(0, 0)
-        turn_slab(3)
         quantise_slab(2)
         h_block(0, 1)
+        turn_slab(3)
         turn_slab(4)
         quantise_slab(3)
         sum_on_scalar(0)
@@ -271,15 +284,14 @@ def tile_graphconvlayer_pa_kernel(tc, x, mask, adj, W0, b0, out):
         h_block(2, 1)
         dinv_step(0, 1)
         h_block(2, 2)
-        dinv_step(0, 2)
         h_block(2, 3)
         normalise(0)
         h_block(3, 0)
         normalise(1)
         quantise_h(2)
-        sum_on_tensor(5)
         h_block(3, 1)
         dinv_step(1, 0)
+        sum_on_tensor(5)
         sum_on_scalar(6)
         turn_tile(0)
         h_block(3, 2)
@@ -288,14 +300,13 @@ def tile_graphconvlayer_pa_kernel(tc, x, mask, adj, W0, b0, out):
         sum_on_tensor(7)
         turn_tile(1)
         sum_on_scalar(8)
-        dinv_step(1, 2)
         quantise_h(3)
         dinv_step(2, 0)
         sum_on_tensor(9)
         quantise_tile(0)
+        sum_on_vector(7)
         dinv_step(2, 1)
         normalise(2)
-        dinv_step(2, 2)
         normalise(3)
         multiply(0)
         quantise_tile(1)
@@ -310,14 +321,15 @@ def tile_graphconvlayer_pa_kernel(tc, x, mask, adj, W0, b0, out):
         turn_tile(5)
         for i in range(2, TILES, 2):
             quantise_tile(i)
-            dinv_step(i // 2 + 2, 2)
-            sum_on_vector(i + 7)
+            sum_on_vector(i + 6)
             normalise(i + 4)
-            dinv_step(i // 2 + 3, 0)
             quantise_tile(i + 1)
-            sum_on_vector(i + 8)
-            dinv_step(i // 2 + 3, 1)
+            sum_on_vector(i + 7)
+            dinv_step(i // 2 + 3, 0)
             normalise(i + 5)
+            dinv_step(i // 2 + 3, 1)
+            sum_on_scalar(i + 8)
+            sum_on_scalar(i + 9)
             multiply(i)
             multiply(i + 1)
             turn_tile(i + 4)

@@ -33,26 +33,23 @@ APART = 8
 FLOPS = 2 * NODES * FEAT * FEAT + 2 * NODES * NODES * FEAT
 
 
-def turn(nc, psum, stage, ident, slab):
+def turn_half(nc, psum, ident, slab, grouped, half):
     words = slab.bitcast(F32)
-    grouped = stage.tile([P, PACK, P, PACK], BF16, tag="grouped", align_bytes=64)
-    for half in range(2):
-        bank = psum.tile([P, 4, P], F32, tag="turned")
-        for j in range(4):
-            first = (4 * half + j) * P
-            nc.tensor.transpose(bank[:, j, :], words[:, first : first + P], ident[:])
-        nc.scalar.copy(
-            out=grouped[:, 2 * half : 2 * half + 2].bitcast(F32),
-            in_=bank[:].rearrange("p (c u) r -> p c r u", u=2),
-        )
-    return grouped
+    bank = psum.tile([P, 4, P], F32, tag="turned")
+    for j in range(4):
+        first = (4 * half + j) * P
+        nc.tensor.transpose(bank[:, j, :], words[:, first : first + P], ident[:])
+    nc.scalar.copy(
+        out=grouped[:, 2 * half : 2 * half + 2].bitcast(F32),
+        in_=bank[:].rearrange("p (c u) r -> p c r u", u=2),
+    )
 
 
 def quantise(nc, grouped, codes, scales):
     nc.vector.quantize_mx(
         out=codes.bitcast(FP8X4),
         scales=scales,
-        in_=grouped[:].rearrange("p c r t -> p (c r t)"),
+        in_=grouped.rearrange("p c r t -> p (c r t)"),
     )
 
 
@@ -99,14 +96,22 @@ def tile_graphconvlayer_pa_kernel(tc, x, mask, adj, W0, b0, out):
         for r in range(FIRST):
             load_pair(r, 2)
         w_raw = raw.tile([P, FEAT // P, FEAT], BF16)
-        for half in range(2):
-            nc.sync.dma_start(out=w_raw[:, 2 * half : 2 * half + 2], in_=w_rows[:, 2 * half : 2 * half + 2, :])
-        slabs = [w_raw[:].rearrange("p a k -> p (a k)")]
-        for c in range(PASSES):
-            x_piece = raw.tile([P, 2, 2 * FEAT], BF16, name="x_raw%d" % c)
+        x_raw = [raw.tile([P, 2, 2 * FEAT], BF16, name="x_raw%d" % c) for c in range(PASSES)]
+        slabs = [w_raw[:].rearrange("p a k -> p (a k)")] + [piece[:].rearrange("p g k -> p (g k)") for piece in x_raw]
+
+        def load_w(half):
+            part = slice(2 * half, 2 * half + 2)
+            nc.sync.dma_start(out=w_raw[:, part], in_=w_rows[:, part, :])
+
+        def load_x(c):
             for u in range(2):
-                nc.sync.dma_start(out=x_piece[:, u], in_=x_rows[:, 2 * c + u, :])
-            slabs.append(x_piece[:].rearrange("p g k -> p (g k)"))
+                nc.sync.dma_start(out=x_raw[c][:, u], in_=x_rows[:, 2 * c + u, :])
+
+        load_w(0)
+        load_x(0)
+        load_w(1)
+        for c in range(1, PASSES):
+            load_x(c)
         mask_bf = const.tile([P, TILES], BF16)
         nc.sync.dma_start(out=mask_bf[:], in_=mask_cols)
         for r in range(FIRST, PAIRS):
@@ -119,11 +124,19 @@ def tile_graphconvlayer_pa_kernel(tc, x, mask, adj, W0, b0, out):
         wx_scales = const.tile([P, 1 + PASSES, FEAT], U8, align_bytes=64)
         wx_grouped = {}
 
-        def turn_slab(s):
-            wx_grouped[s] = turn(nc, psum_turn, stage, ident, slabs[s])
+        def new_grouped():
+            return stage.tile([P, PACK, P, PACK], BF16, tag="grouped", name="grouped", align_bytes=64)
 
-        def quantise_slab(s):
-            quantise(nc, wx_grouped[s], wx_codes[:, s, :], wx_scales[:, s, :])
+        def turn_slab(s, halves=(0, 1)):
+            if s not in wx_grouped:
+                wx_grouped[s] = new_grouped()
+            for half in halves:
+                turn_half(nc, psum_turn, ident, slabs[s], wx_grouped[s], half)
+
+        def quantise_slab(s, half=None):
+            chunks = slice(0, PACK) if half is None else slice(2 * half, 2 * half + 2)
+            cols = slice(P * chunks.start, P * chunks.stop)
+            quantise(nc, wx_grouped[s][:, chunks], wx_codes[:, s, cols], wx_scales[:, s, cols])
 
         deg = [const.tile([P, 2, APART], F32, name="deg%d" % r) for r in range(PAIRS)]
         safe = const.tile([P, PAIRS, 2], F32)
@@ -185,14 +198,16 @@ def tile_graphconvlayer_pa_kernel(tc, x, mask, adj, W0, b0, out):
 
         def turn_tile(i):
             if i < TILES:
-                grouped[i] = turn(nc, psum_turn, stage, ident, adj_n[i][:])
+                grouped[i] = new_grouped()
+                for half in range(2):
+                    turn_half(nc, psum_turn, ident, adj_n[i][:], grouped[i], half)
 
         def quantise_tile(i):
             a_codes = stage.tile([P, PASSES, P], U32, tag="a_codes", align_bytes=64)
             a_scales = stage.tile([P, PASSES, P], U8, tag="a_scales", align_bytes=64)
             quantise(
                 nc,
-                grouped[i],
+                grouped[i][:],
                 a_codes[:].rearrange("p c n -> p (c n)"),
                 a_scales[:].rearrange("p c n -> p (c n)"),
             )
@@ -225,7 +240,7 @@ def tile_graphconvlayer_pa_kernel(tc, x, mask, adj, W0, b0, out):
         def h_block(c, f):
             cols = slice(f * P, (f + 1) * P)
             if f == 0:
-                h_grouped[c] = stage.tile([P, PACK, P, PACK], BF16, tag="grouped", name="h_grouped", align_bytes=64)
+                h_grouped[c] = new_grouped()
             h_ps = psum_sum.tile([P, PACK, P], F32, tag="sums")
             for t in range(PACK):
                 nodes = slice(t * P, (t + 1) * P)
@@ -246,28 +261,30 @@ def tile_graphconvlayer_pa_kernel(tc, x, mask, adj, W0, b0, out):
             )
 
         def quantise_h(c):
-            quantise(nc, h_grouped[c], h_codes[:, c, :], h_scales[:, c, :])
+            quantise(nc, h_grouped[c][:], h_codes[:, c, :], h_scales[:, c, :])
 
         bias_ps = psum_sum.tile([P, FEAT], F32, tag="sums")
         nc.tensor.matmul(out=bias_ps[:], lhsT=ones[:], rhs=bias_row[:], start=True, stop=True)
         bias_all = const.tile([P, FEAT], F32)
         nc.scalar.copy(out=bias_all[:], in_=bias_ps[:])
-        turn_slab(0)
-        quantise_slab(0)
+        turn_slab(0, (0,))
+        quantise_slab(0, 0)
         turn_slab(1)
         quantise_slab(1)
+        turn_slab(0, (1,))
         mask_f = const.tile([P, TILES], F32)
         turn_slab(2)
         h_block(0, 0)
-        quantise_slab(2)
+        quantise_slab(0, 1)
         h_block(0, 1)
         turn_slab(3)
+        quantise_slab(2)
+        h_block(0, 2)
         turn_slab(4)
+        h_block(0, 3)
         quantise_slab(3)
         sum_on_scalar(0)
-        h_block(0, 2)
-        h_block(0, 3)
-        nc.vector.tensor_copy(out=mask_f[:], in_=mask_bf[:])
+        nc.gpsimd.tensor_copy(out=mask_f[:], in_=mask_bf[:])
         h_block(1, 0)
         quantise_h(0)
         sum_on_tensor(1)
@@ -310,10 +327,9 @@ def tile_graphconvlayer_pa_kernel(tc, x, mask, adj, W0, b0, out):
         normalise(3)
         multiply(0)
         quantise_tile(1)
-        dinv_step(3, 0)
         normalise(4)
-        dinv_step(3, 1)
         normalise(5)
+        dinv_step(3, 0)
         turn_tile(2)
         turn_tile(3)
         multiply(1)
@@ -321,13 +337,13 @@ def tile_graphconvlayer_pa_kernel(tc, x, mask, adj, W0, b0, out):
         turn_tile(5)
         for i in range(2, TILES, 2):
             quantise_tile(i)
+            dinv_step(i // 2 + 2, 1)
             sum_on_vector(i + 6)
             normalise(i + 4)
             quantise_tile(i + 1)
             sum_on_vector(i + 7)
-            dinv_step(i // 2 + 3, 0)
             normalise(i + 5)
-            dinv_step(i // 2 + 3, 1)
+            dinv_step(i // 2 + 3, 0)
             sum_on_scalar(i + 8)
             sum_on_scalar(i + 9)
             multiply(i)

@@ -22,8 +22,9 @@ PASSES = NODES // K_PASS
 SLAB = PACK * K_PASS
 
 SHARED_TILES = 10
-ON_SCALAR = (0, 2, 4, 6, 13)
+ON_SCALAR = (0, 2, 4, 8, 13)
 ON_TENSOR = (1, 3, 5, 7, 9)
+SCALED_ON_SCALAR = (0,)
 FIRST = 0
 STAGE_BUFS = 6
 TURN_BANKS = 4
@@ -107,14 +108,21 @@ def tile_graphconvlayer_pa_kernel(tc, x, mask, adj, W0, b0, out):
             for u in range(2):
                 nc.sync.dma_start(out=x_raw[c][:, u], in_=x_rows[:, 2 * c + u, :])
 
+        def load_tile(i):
+            nc.sync.dma_start(out=adj_raw[i // 2][:, i % 2], in_=adj_rows[:, i, :])
+
+        adj_raw.append(raw.tile([P, 2, NODES], BF16, name="adj_raw0"))
         load_w(0)
         load_x(0)
         load_w(1)
-        for c in range(1, PASSES):
-            load_x(c)
+        load_x(1)
+        load_x(2)
+        load_x(3)
+        load_tile(0)
+        load_tile(1)
         mask_bf = const.tile([P, TILES], BF16)
         nc.sync.dma_start(out=mask_bf[:], in_=mask_cols)
-        for r in range(FIRST, PAIRS):
+        for r in range(1, PAIRS):
             load_pair(r)
 
         def adj_tile(i):
@@ -172,16 +180,16 @@ def tile_graphconvlayer_pa_kernel(tc, x, mask, adj, W0, b0, out):
                     op0=ALU.mult, op1=ALU.add, accum_out=deg_of(i),
                 )
 
-        def dinv_step(r, step):
+        def dinv_step(r, step, w=slice(0, 2)):
             if not 0 <= r < PAIRS:
                 return
-            d = deg[r][:, :, 0]
+            d = deg[r][:, w, 0]
             if step == 0:
                 nc.vector.scalar_tensor_tensor(
-                    out=safe[:, r, :], in0=d, scalar=0.0, in1=d, op0=ALU.is_equal, op1=ALU.add
+                    out=safe[:, r, w], in0=d, scalar=0.0, in1=d, op0=ALU.is_equal, op1=ALU.add
                 )
             elif step == 1:
-                nc.vector.reciprocal(out=dinv[:, r, :], in_=safe[:, r, :])
+                nc.vector.reciprocal(out=dinv[:, r, w], in_=safe[:, r, w])
 
         adj_n = {}
         grouped = {}
@@ -191,9 +199,12 @@ def tile_graphconvlayer_pa_kernel(tc, x, mask, adj, W0, b0, out):
             if i < TILES:
                 scaled = stage.tile([P, NODES], BF16, tag="adj_n")
                 factor = dinv[:, i // 2, i % 2 : i % 2 + 1]
-                nc.vector.tensor_scalar(
-                    out=scaled[:], in0=adj_tile(i), scalar1=factor, scalar2=None, op0=ALU.mult
-                )
+                if i in SCALED_ON_SCALAR:
+                    nc.scalar.activation(out=scaled[:], in_=adj_tile(i), func=ACT.Copy, scale=factor)
+                else:
+                    nc.vector.tensor_scalar(
+                        out=scaled[:], in0=adj_tile(i), scalar1=factor, scalar2=None, op0=ALU.mult
+                    )
                 adj_n[i] = scaled
 
         def turn_tile(i):
@@ -293,16 +304,16 @@ def tile_graphconvlayer_pa_kernel(tc, x, mask, adj, W0, b0, out):
         quantise_slab(4)
         h_block(1, 2)
         h_block(1, 3)
+        dinv_step(0, 0)
         h_block(2, 0)
+        dinv_step(0, 1)
         quantise_h(1)
         sum_on_tensor(3)
+        normalise(0)
         sum_on_scalar(4)
-        dinv_step(0, 0)
         h_block(2, 1)
-        dinv_step(0, 1)
         h_block(2, 2)
         h_block(2, 3)
-        normalise(0)
         h_block(3, 0)
         normalise(1)
         quantise_h(2)
@@ -321,13 +332,13 @@ def tile_graphconvlayer_pa_kernel(tc, x, mask, adj, W0, b0, out):
         dinv_step(2, 0)
         sum_on_tensor(9)
         quantise_tile(0)
-        sum_on_vector(7)
         dinv_step(2, 1)
         normalise(2)
         normalise(3)
         multiply(0)
         quantise_tile(1)
         normalise(4)
+        sum_on_vector(6)
         normalise(5)
         dinv_step(3, 0)
         turn_tile(2)

@@ -22,7 +22,7 @@ PASSES = NODES // K_PASS
 SLAB = PACK * K_PASS
 
 SHARED_TILES = 10
-ON_SCALAR = (0, 2, 4, 8, 13)
+ON_SCALAR = (0, 2, 4, 8, 14)
 ON_TENSOR = (1, 3, 5, 7, 9)
 SCALED_ON_SCALAR = (0,)
 FIRST = 0

@@ -21,6 +21,7 @@ PAIRS = TILES // 2
 PASSES = NODES // K_PASS
 SLAB = PACK * K_PASS
 
+LAST_WIDTHS = (256, 128, 128)
 SHARED_TILES = 10
 ON_SCALAR = (0, 2, 4, 8, 14)
 ON_TENSOR = (1, 3, 5, 7, 9)
@@ -226,10 +227,10 @@ def tile_graphconvlayer_pa_kernel(tc, x, mask, adj, W0, b0, out):
 
         def multiply(i):
             a_codes, a_scales = codes[i]
-            pieces = 2 if i == TILES - 1 else 1
-            for piece in range(pieces):
-                cols = slice(piece * FEAT // pieces, (piece + 1) * FEAT // pieces)
-                z_ps = psum_sum.tile([P, FEAT // pieces], F32, tag="sums")
+            widths = LAST_WIDTHS if i == TILES - 1 else (FEAT,)
+            for k, width in enumerate(widths):
+                cols = slice(sum(widths[:k]), sum(widths[: k + 1]))
+                z_ps = psum_sum.tile([P, width], F32, tag="sums")
                 for c in range(PASSES):
                     nc.tensor.matmul_mx(
                         out=z_ps[:],
@@ -240,7 +241,7 @@ def tile_graphconvlayer_pa_kernel(tc, x, mask, adj, W0, b0, out):
                         start=(c == 0),
                         stop=(c == PASSES - 1),
                     )
-                result = stage.tile([P, FEAT // pieces], F32, tag="result")
+                result = stage.tile([P, width], F32, tag="result")
                 nc.scalar.activation(out=result[:], in_=z_ps[:], func=ACT.Gelu, scale=mask_f[:, i : i + 1])
                 nc.sync.dma_start(out=out_rows[:, i, cols], in_=result[:])
 
@@ -295,10 +296,10 @@ def tile_graphconvlayer_pa_kernel(tc, x, mask, adj, W0, b0, out):
         h_block(0, 3)
         quantise_slab(3)
         sum_on_scalar(0)
-        nc.gpsimd.tensor_copy(out=mask_f[:], in_=mask_bf[:])
         h_block(1, 0)
         quantise_h(0)
         sum_on_tensor(1)
+        nc.scalar.copy(out=mask_f[:], in_=mask_bf[:])
         sum_on_scalar(2)
         h_block(1, 1)
         quantise_slab(4)
@@ -328,23 +329,23 @@ def tile_graphconvlayer_pa_kernel(tc, x, mask, adj, W0, b0, out):
         sum_on_tensor(7)
         turn_tile(1)
         sum_on_scalar(8)
+        normalise(2)
         quantise_h(3)
         dinv_step(2, 0)
         sum_on_tensor(9)
         quantise_tile(0)
         dinv_step(2, 1)
-        normalise(2)
         normalise(3)
+        turn_tile(2)
         multiply(0)
         quantise_tile(1)
         normalise(4)
         sum_on_vector(6)
         normalise(5)
         dinv_step(3, 0)
-        turn_tile(2)
         turn_tile(3)
-        multiply(1)
         turn_tile(4)
+        multiply(1)
         turn_tile(5)
         for i in range(2, TILES, 2):
             quantise_tile(i)

from contextlib import ExitStack

import concourse.masks as masks
import concourse.mybir as mybir

F32 = mybir.dt.float32
BF16 = mybir.dt.bfloat16
U32 = mybir.dt.uint32
U8 = mybir.dt.uint8
FP8X4 = mybir.dt.float8_e4m3fn_x4
ALU = mybir.AluOpType
ACT = mybir.ActivationFunctionType

P = 128
PACK = 4
K_PASS = P * PACK
NODES = 2048
FEAT = 512
TILES = NODES // P
PAIRS = TILES // 2
PASSES = NODES // K_PASS
SLAB = PACK * K_PASS

LAST_WIDTHS = (256, 128, 128)
SHARED_TILES = 10
ON_SCALAR = (0, 2, 4, 8, 14)
ON_TENSOR = (1, 3, 5, 7, 9)
SCALED_ON_SCALAR = (0,)
FIRST = 0
STAGE_BUFS = 6
TURN_BANKS = 4
SUM_BANKS = 4
APART = 8

FLOPS = 2 * NODES * FEAT * FEAT + 2 * NODES * NODES * FEAT


def turn_half(nc, psum, ident, slab, grouped, half):
    words = slab.bitcast(F32)
    bank = psum.tile([P, 4, P], F32, tag="turned")
    for j in range(4):
        first = (4 * half + j) * P
        nc.tensor.transpose(bank[:, j, :], words[:, first : first + P], ident[:])
    nc.scalar.copy(
        out=grouped[:, 2 * half : 2 * half + 2].bitcast(F32),
        in_=bank[:].rearrange("p (c u) r -> p c r u", u=2),
    )


def quantise(nc, grouped, codes, scales):
    nc.vector.quantize_mx(
        out=codes.bitcast(FP8X4),
        scales=scales,
        in_=grouped.rearrange("p c r t -> p (c r t)"),
    )


def tile_graphconvlayer_pa_kernel(tc, x, mask, adj, W0, b0, out):
    nc = tc.nc
    adj_rows = adj[0].rearrange("(p i) m -> p i m", i=TILES)
    out_rows = out[0].rearrange("(p i) o -> p i o", i=TILES)
    mask_cols = mask[0].rearrange("(p i) -> p i", i=TILES)
    x_rows = x[0].rearrange("(g q e) k -> q g (e k)", q=P, e=2)
    w_rows = W0.rearrange("(a r) k -> r a k", r=P)

    with ExitStack() as ctx:
        const = ctx.enter_context(tc.tile_pool(name="const", bufs=1))
        raw = ctx.enter_context(tc.tile_pool(name="raw", bufs=1))
        stage = ctx.enter_context(tc.tile_pool(name="stage", bufs=STAGE_BUFS))
        psum_turn = ctx.enter_context(tc.psum_pool(name="psum_turn", bufs=TURN_BANKS))
        psum_sum = ctx.enter_context(tc.psum_pool(name="psum_sum", bufs=SUM_BANKS))
        ctx.enter_context(tc.manual_schedule())

        ident = const.tile([P, P], F32)
        masks.make_identity(nc, ident[:])
        ident_bf = const.tile([P, P], BF16)
        masks.make_identity(nc, ident_bf[:])
        ones = const.tile([P, P], BF16)
        nc.vector.memset(ones[:], 1.0)
        bias_row = const.tile([P, FEAT], BF16)
        nc.vector.memset(bias_row[:], 0.0)
        warm = const.tile([P, 1], F32)
        nc.vector.memset(warm[:], 0.0)
        nc.scalar.activation(out=warm[:], in_=warm[:], func=ACT.Gelu)

        nc.sync.dma_start(out=bias_row[0:1, :], in_=b0.unsqueeze(0))
        adj_raw = []

        def load_pair(r, pieces=1):
            adj_pair = raw.tile([P, 2, NODES], BF16, name="adj_raw%d" % r)
            for w in range(pieces):
                part = slice(2 * w // pieces, 2 * (w + 1) // pieces)
                nc.sync.dma_start(
                    out=adj_pair[:, part], in_=adj_rows[:, 2 * r + part.start : 2 * r + part.stop, :]
                )
            adj_raw.append(adj_pair)

        for r in range(FIRST):
            load_pair(r, 2)
        w_raw = raw.tile([P, FEAT // P, FEAT], BF16)
        x_raw = [raw.tile([P, 2, 2 * FEAT], BF16, name="x_raw%d" % c) for c in range(PASSES)]
        slabs = [w_raw[:].rearrange("p a k -> p (a k)")] + [piece[:].rearrange("p g k -> p (g k)") for piece in x_raw]

        def load_w(half):
            part = slice(2 * half, 2 * half + 2)
            nc.sync.dma_start(out=w_raw[:, part], in_=w_rows[:, part, :])

        def load_x(c):
            for u in range(2):
                nc.sync.dma_start(out=x_raw[c][:, u], in_=x_rows[:, 2 * c + u, :])

        def load_tile(i):
            nc.sync.dma_start(out=adj_raw[i // 2][:, i % 2], in_=adj_rows[:, i, :])

        adj_raw.append(raw.tile([P, 2, NODES], BF16, name="adj_raw0"))
        load_w(0)
        load_x(0)
        load_w(1)
        load_x(1)
        load_x(2)
        load_x(3)
        load_tile(0)
        load_tile(1)
        mask_bf = const.tile([P, TILES], BF16)
        nc.sync.dma_start(out=mask_bf[:], in_=mask_cols)
        for r in range(1, PAIRS):
            load_pair(r)

        def adj_tile(i):
            return adj_raw[i // 2][:, i % 2, :]

        wx_codes = const.tile([P, 1 + PASSES, FEAT], U32, align_bytes=64)
        wx_scales = const.tile([P, 1 + PASSES, FEAT], U8, align_bytes=64)
        wx_grouped = {}

        def new_grouped():
            return stage.tile([P, PACK, P, PACK], BF16, tag="grouped", name="grouped", align_bytes=64)

        def turn_slab(s, halves=(0, 1)):
            if s not in wx_grouped:
                wx_grouped[s] = new_grouped()
            for half in halves:
                turn_half(nc, psum_turn, ident, slabs[s], wx_grouped[s], half)

        def quantise_slab(s, half=None):
            chunks = slice(0, PACK) if half is None else slice(2 * half, 2 * half + 2)
            cols = slice(P * chunks.start, P * chunks.stop)
            quantise(nc, wx_grouped[s][:, chunks], wx_codes[:, s, cols], wx_scales[:, s, cols])

        deg = [const.tile([P, 2, APART], F32, name="deg%d" % r) for r in range(PAIRS)]
        safe = const.tile([P, PAIRS, 2], F32)
        dinv = const.tile([P, PAIRS, 2], F32)

        def deg_of(i):
            return deg[i // 2][:, i % 2, 0:1]

        def sum_on_tensor(i):
            if i in ON_TENSOR:
                fold = psum_turn.tile([P, 4, P], F32, tag="turned", name="fold")
                for j in range(NODES // P):
                    nc.tensor.matmul(
                        out=fold[:, 0, :],
                        lhsT=ident_bf[:],
                        rhs=adj_tile(i)[:, j * P : (j + 1) * P],
                        start=(j == 0),
                        stop=(j == NODES // P - 1),
                    )
                unread_f = stage.tile([P, P], F32, tag="unread_f", bufs=1)
                nc.scalar.activation(out=unread_f[:], in_=fold[:, 0, :], func=ACT.Copy, accum_out=deg_of(i))

        def sum_on_scalar(i):
            if i in ON_SCALAR:
                unread_s = stage.tile([P, NODES], BF16, tag="unread_s", bufs=1)
                nc.scalar.activation(out=unread_s[:], in_=adj_tile(i), func=ACT.Copy, accum_out=deg_of(i))

        def sum_on_vector(i):
            if i < TILES and i not in ON_SCALAR and i not in ON_TENSOR:
                unread_v = stage.tile([P, NODES], BF16, tag="unread_v", bufs=1)
                nc.vector.tensor_scalar(
                    out=unread_v[:], in0=adj_tile(i), scalar1=1.0, scalar2=None,
                    op0=ALU.mult, op1=ALU.add, accum_out=deg_of(i),
                )

        def dinv_step(r, step, w=slice(0, 2)):
            if not 0 <= r < PAIRS:
                return
            d = deg[r][:, w, 0]
            if step == 0:
                nc.vector.scalar_tensor_tensor(
                    out=safe[:, r, w], in0=d, scalar=0.0, in1=d, op0=ALU.is_equal, op1=ALU.add
                )
            elif step == 1:
                nc.vector.reciprocal(out=dinv[:, r, w], in_=safe[:, r, w])

        adj_n = {}
        grouped = {}
        codes = {}

        def normalise(i):
            if i < TILES:
                scaled = stage.tile([P, NODES], BF16, tag="adj_n")
                factor = dinv[:, i // 2, i % 2 : i % 2 + 1]
                if i in SCALED_ON_SCALAR:
                    nc.scalar.activation(out=scaled[:], in_=adj_tile(i), func=ACT.Copy, scale=factor)
                else:
                    nc.vector.tensor_scalar(
                        out=scaled[:], in0=adj_tile(i), scalar1=factor, scalar2=None, op0=ALU.mult
                    )
                adj_n[i] = scaled

        def turn_tile(i):
            if i < TILES:
                grouped[i] = new_grouped()
                for half in range(2):
                    turn_half(nc, psum_turn, ident, adj_n[i][:], grouped[i], half)

        def quantise_tile(i):
            a_codes = stage.tile([P, PASSES, P], U32, tag="a_codes", align_bytes=64)
            a_scales = stage.tile([P, PASSES, P], U8, tag="a_scales", align_bytes=64)
            quantise(
                nc,
                grouped[i][:],
                a_codes[:].rearrange("p c n -> p (c n)"),
                a_scales[:].rearrange("p c n -> p (c n)"),
            )
            codes[i] = (a_codes, a_scales)

        def multiply(i):
            a_codes, a_scales = codes[i]
            widths = LAST_WIDTHS if i == TILES - 1 else (FEAT,)
            for k, width in enumerate(widths):
                cols = slice(sum(widths[:k]), sum(widths[: k + 1]))
                z_ps = psum_sum.tile([P, width], F32, tag="sums")
                for c in range(PASSES):
                    nc.tensor.matmul_mx(
                        out=z_ps[:],
                        lhsT=a_codes[:, c, :].bitcast(FP8X4),
                        lhsT_scale=a_scales[:, c, :],
                        rhs=h_codes[:, c, cols].bitcast(FP8X4),
                        rhs_scale=h_scales[:, c, cols],
                        start=(c == 0),
                        stop=(c == PASSES - 1),
                    )
                result = stage.tile([P, width], F32, tag="result")
                nc.scalar.activation(out=result[:], in_=z_ps[:], func=ACT.Gelu, scale=mask_f[:, i : i + 1])
                nc.sync.dma_start(out=out_rows[:, i, cols], in_=result[:])

        h_codes = const.tile([P, PASSES, FEAT], U32, align_bytes=64)
        h_scales = const.tile([P, PASSES, FEAT], U8, align_bytes=64)
        h_grouped = {}

        def h_block(c, f):
            cols = slice(f * P, (f + 1) * P)
            if f == 0:
                h_grouped[c] = new_grouped()
            h_ps = psum_sum.tile([P, PACK, P], F32, tag="sums")
            for t in range(PACK):
                nodes = slice(t * P, (t + 1) * P)
                nc.tensor.matmul_mx(
                    out=h_ps[:, t, :],
                    lhsT=wx_codes[:, 1 + c, nodes].bitcast(FP8X4),
                    lhsT_scale=wx_scales[:, 1 + c, nodes],
                    rhs=wx_codes[:, 0, cols].bitcast(FP8X4),
                    rhs_scale=wx_scales[:, 0, cols],
                    start=True,
                    stop=True,
                )
            nc.vector.tensor_tensor(
                out=h_grouped[c][:, f],
                in0=h_ps[:].rearrange("p t o -> p o t"),
                in1=bias_all[:, cols].unsqueeze(2).to_broadcast([P, P, PACK]),
                op=ALU.add,
            )

        def quantise_h(c):
            quantise(nc, h_grouped[c][:], h_codes[:, c, :], h_scales[:, c, :])

        bias_ps = psum_sum.tile([P, FEAT], F32, tag="sums")
        nc.tensor.matmul(out=bias_ps[:], lhsT=ones[:], rhs=bias_row[:], start=True, stop=True)
        bias_all = const.tile([P, FEAT], F32)
        nc.scalar.copy(out=bias_all[:], in_=bias_ps[:])
        turn_slab(0, (0,))
        quantise_slab(0, 0)
        turn_slab(1)
        quantise_slab(1)
        turn_slab(0, (1,))
        mask_f = const.tile([P, TILES], F32)
        turn_slab(2)
        h_block(0, 0)
        quantise_slab(0, 1)
        h_block(0, 1)
        turn_slab(3)
        quantise_slab(2)
        h_block(0, 2)
        turn_slab(4)
        h_block(0, 3)
        quantise_slab(3)
        sum_on_scalar(0)
        h_block(1, 0)
        quantise_h(0)
        sum_on_tensor(1)
        nc.scalar.copy(out=mask_f[:], in_=mask_bf[:])
        sum_on_scalar(2)
        h_block(1, 1)
        quantise_slab(4)
        h_block(1, 2)
        h_block(1, 3)
        dinv_step(0, 0)
        h_block(2, 0)
        dinv_step(0, 1)
        quantise_h(1)
        sum_on_tensor(3)
        normalise(0)
        sum_on_scalar(4)
        h_block(2, 1)
        h_block(2, 2)
        h_block(2, 3)
        h_block(3, 0)
        normalise(1)
        quantise_h(2)
        h_block(3, 1)
        dinv_step(1, 0)
        sum_on_tensor(5)
        sum_on_scalar(6)
        turn_tile(0)
        h_block(3, 2)
        dinv_step(1, 1)
        h_block(3, 3)
        sum_on_tensor(7)
        turn_tile(1)
        sum_on_scalar(8)
        normalise(2)
        quantise_h(3)
        dinv_step(2, 0)
        sum_on_tensor(9)
        quantise_tile(0)
        dinv_step(2, 1)
        normalise(3)
        turn_tile(2)
        multiply(0)
        quantise_tile(1)
        normalise(4)
        sum_on_vector(6)
        normalise(5)
        dinv_step(3, 0)
        turn_tile(3)
        turn_tile(4)
        multiply(1)
        turn_tile(5)
        for i in range(2, TILES, 2):
            quantise_tile(i)
            dinv_step(i // 2 + 2, 1)
            sum_on_vector(i + 6)
            normalise(i + 4)
            quantise_tile(i + 1)
            sum_on_vector(i + 7)
            normalise(i + 5)
            dinv_step(i // 2 + 3, 0)
            sum_on_scalar(i + 8)
            sum_on_scalar(i + 9)
            multiply(i)
            multiply(i + 1)
            turn_tile(i + 4)
            turn_tile(i + 5)
